import numpy as np
import ml_dtypes


def mxq(x, axis, fmt="e4m3"):
    dtype, down = {"e4m3": (ml_dtypes.float8_e4m3fn, 7), "e5m2": (ml_dtypes.float8_e5m2, 14)}[fmt]
    v = np.moveaxis(np.asarray(x, np.float32).astype(ml_dtypes.bfloat16).astype(np.float64), axis, -1)
    blocks = v.reshape(v.shape[:-1] + (-1, 32))
    amax = np.abs(blocks).max(-1, keepdims=True)
    byte = np.maximum(np.where(amax > 0, np.frexp(amax)[1] - 1 + 127, 0) - down, 1)
    scale = np.exp2(byte - 127.0)
    codes = (blocks / scale).astype(np.float32).astype(dtype).astype(np.float64)
    return np.moveaxis((codes * scale).reshape(v.shape), -1, axis)


WIDE = False


def mx_kscale(k):
    if not WIDE:
        return np.ones(k)
    levels = np.array([10, -10, 5, -5, 0])
    a = np.random.permutation(np.resize(levels, k // 512 * 4)).reshape(k // 512, 4)
    idx = np.arange(k)
    return np.exp2(a[idx // 512, idx % 128 // 32])


BF16 = ml_dtypes.bfloat16


def bf(x):
    return np.asarray(x, np.float32).astype(BF16)


def f64(x):
    return np.asarray(x).astype(np.float64)


B, S, D, E, WINDOW = 2, 512, 1024, 1024, 10
HALF = WINDOW // 2
NW = HALF + HALF + 1


def setup_inputs():
    s, t = mx_kscale(D), mx_kscale(E)
    pos = np.arange(S)[:, None] + np.arange(NW)[None, :] - HALF
    e = np.exp(np.random.standard_normal((B, S, NW))) * ((pos >= 0) & (pos < S))
    return {"x": bf(np.random.standard_normal((B, S, D)) * s),
            "Wv": bf(np.random.standard_normal((E, D)) / np.sqrt(D) / s[None, :] * t[:, None]),
            "bv": bf(np.random.standard_normal(E) * 0.1 * t),
            "attn_band": bf(e / e.sum(-1, keepdims=True)),
            "Wo": bf(np.random.standard_normal((D, E)) / np.sqrt(E) / t[None, :]),
            "bo": bf(np.random.standard_normal(D) * 0.1)}


def reference(x, Wv, bv, attn_band, Wo, bo):
    v = (mxq(f64(x), 2, "e4m3") @ mxq(f64(Wv), 1, "e4m3").T) + f64(bv)
    a = f64(attn_band)
    ctx = np.zeros((B, S, E))
    for o in range(NW):
        sh = o - HALF
        lo, hi = max(0, -sh), min(S, S - sh)
        ctx[:, lo:hi] += a[:, lo:hi, o:o + 1] * v[:, lo + sh:hi + sh]
    return (mxq(ctx, 2, "e4m3") @ mxq(f64(Wo), 1, "e4m3").T) + f64(bo)

@@ -1,0 +1,279 @@
+from contextlib import ExitStack
+
+import concourse.mybir as mybir
+from concourse.masks import make_identity
+
+F32 = mybir.dt.float32
+BF16 = mybir.dt.bfloat16
+U32 = mybir.dt.uint32
+U8 = mybir.dt.uint8
+FP8X4 = mybir.dt.float8_e4m3fn_x4
+ADD = mybir.AluOpType.add
+
+P = 128
+PACK = 4
+BATCH, SEQ, FEATURES = 2, 512, 1024
+TAPS, HALF = 11, 5
+TAP_SLOT = 16
+PASSES = FEATURES // (P * PACK)
+BLOCKS = FEATURES // P
+N_TILE = 512
+HALVES = FEATURES // N_TILE
+
+WIN_STEP = 96
+MARGIN = (P - WIN_STEP) // 2
+WINS = (SEQ - P) // WIN_STEP + 1
+N_WINDOWS = BATCH * WINS
+
+ROW_PITCH = 136
+
+LEAD = 3
+X_BEFORE_WO = LEAD + 3
+
+FLOPS = 2 * 2 * BATCH * SEQ * FEATURES * FEATURES + 2 * BATCH * SEQ * TAPS * FEATURES
+
+
+def window_place(w):
+    b, s = divmod(w, WINS)
+    lo = 0 if s == 0 else MARGIN
+    hi = P if s == WINS - 1 else P - MARGIN
+    return b, s * WIN_STEP, lo, hi
+
+
+def tile_localattention_pb_kernel(tc, x, Wv, bv, attn_band, Wo, bo, out):
+    nc = tc.nc
+    out_rows_hbm = out.rearrange("b s d -> (b s) d")
+    out_flat = out.rearrange("b s d -> (b s d)")
+
+    with ExitStack() as stack:
+        keep = stack.enter_context(tc.tile_pool(name="keep", bufs=1))
+        x_pool = stack.enter_context(tc.tile_pool(name="x_pool", bufs=N_WINDOWS))
+        pairs_pool = stack.enter_context(tc.tile_pool(name="pairs_pool", bufs=3))
+        v_pool = stack.enter_context(tc.tile_pool(name="v_pool", bufs=LEAD + 1))
+        out_pool = stack.enter_context(tc.tile_pool(name="out_pool", bufs=4))
+        psum = stack.enter_context(tc.psum_pool(name="psum", bufs=2))
+        stack.enter_context(tc.manual_schedule())
+
+        weights_win = keep.tile([P, N_WINDOWS, TAP_SLOT], BF16)
+        for b in range(BATCH):
+            wins = slice(b * WINS, (b + 1) * WINS)
+            nc.sync.dma_start(
+                out=weights_win[0:WIN_STEP, wins, 0:TAPS],
+                in_=attn_band[b, 0 : WINS * WIN_STEP, :].rearrange("(s r) o -> r s o", r=WIN_STEP),
+            )
+            nc.sync.dma_start(
+                out=weights_win[WIN_STEP:P, wins, 0:TAPS],
+                in_=attn_band[b, P - WIN_STEP : SEQ, :].rearrange("(s r) o -> r s o", r=WIN_STEP)[
+                    2 * WIN_STEP - P : WIN_STEP
+                ],
+            )
+
+        x_rows = {}
+
+        def load_x(w):
+            b, first, lo, hi = window_place(w)
+            x_win = x_pool.tile([P, FEATURES], BF16)
+            nc.sync.dma_start(out=x_win[:], in_=x[b, first : first + P, :])
+            x_rows[w] = x_win
+
+        load_x(0)
+        wv_rows = keep.tile([P, BLOCKS, FEATURES], BF16)
+        for q in range(BLOCKS // 2):
+            nc.sync.dma_start(
+                out=wv_rows[:, 2 * q : 2 * q + 2, :],
+                in_=Wv[2 * P * q : 2 * P * (q + 1), :].rearrange("(m e) k -> m e k", e=2),
+            )
+        bv_all = keep.tile([P, FEATURES], BF16)
+        nc.sync.dma_start(out=bv_all[:], in_=bv.partition_broadcast(P))
+        for w in range(1, X_BEFORE_WO):
+            load_x(w)
+        wo_rows = keep.tile([P, BLOCKS, FEATURES], BF16)
+        for q in range(BLOCKS // 2):
+            nc.sync.dma_start(
+                out=wo_rows[:, 2 * q : 2 * q + 2, :],
+                in_=Wo[2 * P * q : 2 * P * (q + 1), :].rearrange("(j m) k -> m j k", m=P),
+            )
+        bo_all = keep.tile([P, FEATURES], BF16)
+        nc.sync.dma_start(out=bo_all[:], in_=bo.partition_broadcast(P))
+        for w in range(X_BEFORE_WO, N_WINDOWS):
+            load_x(w)
+
+        ident = keep.tile([P, P], F32)
+        make_identity(nc, ident[:])
+
+        total = BATCH * SEQ * FEATURES
+        parked = out_flat[total - N_WINDOWS * P * ROW_PITCH : total]
+        padded = keep.tile([P, N_WINDOWS, ROW_PITCH], F32)
+        nc.vector.memset(padded[:], 0.0)
+        nc.vector.tensor_copy(out=padded[:, :, 0:TAPS], in_=weights_win[:, :, 0:TAPS])
+        nc.gpsimd.dma_start(
+            out=parked.rearrange("(w p q) -> p w q", p=P, q=ROW_PITCH), in_=padded[:]
+        )
+        band = keep.tile([P, N_WINDOWS, P], F32)
+        nc.gpsimd.dma_start(
+            out=band[:],
+            in_=parked.rearrange("(w r) -> w r", r=P * ROW_PITCH)[
+                :, HALF : HALF + P * (ROW_PITCH - 1)
+            ].rearrange("w (p q) -> p w q", q=ROW_PITCH - 1)[:, :, 0:P],
+        )
+        band_t = keep.tile([P, N_WINDOWS, P], F32)
+
+        def transpose_band():
+            for w0 in range(0, N_WINDOWS, PACK):
+                count = min(PACK, N_WINDOWS - w0)
+                flipped = psum.tile([P, PACK, P], F32, tag="flipped")
+                for j in range(count):
+                    nc.tensor.transpose(flipped[:, j, :], band[:, w0 + j, :], ident[:])
+                nc.scalar.copy(out=band_t[:, w0 : w0 + count, :], in_=flipped[:, 0:count, :])
+
+        def transpose_rows(rows, pairs, copy):
+            words = rows.bitcast(F32)
+            flipped = psum.tile([P, PACK, P], F32, tag="flipped")
+            for j in range(PACK):
+                nc.tensor.transpose(flipped[:, j, :], words[:, j * P : (j + 1) * P], ident[:])
+            copy(out=pairs, in_=flipped[:].rearrange("p (c u) r -> p c r u", u=2))
+
+        x_codes = keep.tile([P, N_WINDOWS, PASSES, P], U32, align_bytes=64)
+        x_scales = keep.tile([P, N_WINDOWS, PASSES, P], U8, align_bytes=64)
+
+        def prepare_x(w):
+            x_pairs = pairs_pool.tile([P, PASSES * P * 2], F32, align_bytes=64)
+            transpose_rows(
+                x_rows[w][:],
+                x_pairs[:].rearrange("p (c r u) -> p c r u", c=PASSES, u=2),
+                nc.scalar.copy,
+            )
+            nc.vector.quantize_mx(
+                out=x_codes[:, w, :, :].rearrange("p c r -> p (c r)").bitcast(FP8X4),
+                scales=x_scales[:, w, :, :].rearrange("p c r -> p (c r)"),
+                in_=x_pairs[:].bitcast(BF16),
+            )
+
+        def weight_tiles(label):
+            pairs = keep.tile([P, PASSES, FEATURES, 2], F32, name=label + "_pairs", align_bytes=64)
+            codes = keep.tile([P, PASSES, FEATURES], U32, name=label + "_codes", align_bytes=64)
+            scales = keep.tile([P, PASSES, FEATURES], U8, name=label + "_scales", align_bytes=64)
+            return pairs, codes, scales
+
+        def prepare_weight_half(rows, tiles, half):
+            pairs, codes, scales = tiles
+            for blk in range(half * PACK, (half + 1) * PACK):
+                copy = nc.scalar.copy if blk % 2 == 0 else nc.vector.tensor_copy
+                transpose_rows(rows[:, blk, :], pairs[:, :, blk * P : (blk + 1) * P, :], copy)
+            cols = slice(half * N_TILE, (half + 1) * N_TILE)
+            for c in range(PASSES):
+                nc.vector.quantize_mx(
+                    out=codes[:, c, cols].bitcast(FP8X4),
+                    scales=scales[:, c, cols],
+                    in_=pairs[:, c, cols, :].rearrange("p n u -> p (n u)").bitcast(BF16),
+                )
+
+        wv_tiles = weight_tiles("wv")
+        wo_tiles = weight_tiles("wo")
+
+        def product(acc, left_codes, left_scales, tiles, half):
+            pairs, codes, scales = tiles
+            cols = slice(half * N_TILE, (half + 1) * N_TILE)
+            for c in range(PASSES):
+                nc.tensor.matmul_mx(
+                    out=acc,
+                    lhsT=left_codes[c].bitcast(FP8X4),
+                    lhsT_scale=left_scales[c],
+                    rhs=codes[:, c, cols].bitcast(FP8X4),
+                    rhs_scale=scales[:, c, cols],
+                    start=(c == 0),
+                    stop=(c == PASSES - 1),
+                )
+
+        v_rows = {}
+
+        def project_v(w):
+            v_win = v_pool.tile([P, FEATURES], F32)
+            for half in range(HALVES):
+                cols = slice(half * N_TILE, (half + 1) * N_TILE)
+                v_acc = psum.tile([P, N_TILE], F32)
+                product(
+                    v_acc[:],
+                    [x_codes[:, w, c, :] for c in range(PASSES)],
+                    [x_scales[:, w, c, :] for c in range(PASSES)],
+                    wv_tiles,
+                    half,
+                )
+                nc.vector.tensor_tensor(
+                    out=v_win[:, cols].rearrange("p (u e m) -> p u e m", u=2, e=2),
+                    in0=v_acc[:].rearrange("p (u e m) -> p u e m", u=2, e=2),
+                    in1=bv_all[:, cols].rearrange("p (u m e) -> p u e m", u=2, e=2),
+                    op=ADD,
+                )
+            v_rows[w] = v_win
+
+        ctx_quads = keep.tile([P, PASSES, BATCH * SEQ, PACK], BF16, align_bytes=64)
+        ctx_codes = keep.tile([P, PASSES, BATCH * SEQ], U32, align_bytes=64)
+        ctx_scales = keep.tile([P, PASSES, BATCH * SEQ], U8, align_bytes=64)
+
+        def mix(w):
+            b, first, lo, hi = window_place(w)
+            token = b * SEQ + first + lo
+            for c in range(PASSES):
+                mix_acc = psum.tile([P, PACK, P], F32)
+                for t in range(PACK):
+                    blk = c * PACK + t
+                    nc.tensor.matmul(
+                        out=mix_acc[:, t, 0 : hi - lo],
+                        lhsT=v_rows[w][:, blk * P : (blk + 1) * P],
+                        rhs=band_t[:, w, lo:hi],
+                        start=True,
+                        stop=True,
+                    )
+                nc.scalar.copy(
+                    out=ctx_quads[:, c, token : token + hi - lo, :],
+                    in_=mix_acc[:, :, 0 : hi - lo].rearrange("p t i -> p i t"),
+                )
+
+        def quantise_ctx(tb):
+            tokens = slice(tb * P, (tb + 1) * P)
+            for c in range(PASSES):
+                nc.vector.quantize_mx(
+                    out=ctx_codes[:, c, tokens].bitcast(FP8X4),
+                    scales=ctx_scales[:, c, tokens],
+                    in_=ctx_quads[:, c, tokens, :].rearrange("p i t -> p (i t)"),
+                )
+
+        def project_out(tb):
+            tokens = slice(tb * P, (tb + 1) * P)
+            for half in range(HALVES):
+                cols = slice(half * N_TILE, (half + 1) * N_TILE)
+                out_acc = psum.tile([P, N_TILE], F32)
+                product(
+                    out_acc[:],
+                    [ctx_codes[:, c, tokens] for c in range(PASSES)],
+                    [ctx_scales[:, c, tokens] for c in range(PASSES)],
+                    wo_tiles,
+                    half,
+                )
+                out_sb = out_pool.tile([P, N_TILE], F32)
+                nc.vector.tensor_tensor(out=out_sb[:], in0=out_acc[:], in1=bo_all[:, cols], op=ADD)
+                nc.sync.dma_start(out=out_rows_hbm[tokens, cols], in_=out_sb[:])
+
+        prepare_x(0)
+        for half in range(HALVES):
+            prepare_weight_half(wv_rows, wv_tiles, half)
+        prepare_x(1)
+
+        for step in range(N_WINDOWS + LEAD + 1):
+            if step < N_WINDOWS:
+                project_v(step)
+            b, s = divmod(step - LEAD - 1, WINS)
+            if step - LEAD - 1 >= 0 and s >= 1:
+                project_out(b * (SEQ // P) + s - 1)
+            if 0 <= step - LEAD < N_WINDOWS:
+                mix(step - LEAD)
+                b, s = divmod(step - LEAD, WINS)
+                if s >= 1:
+                    quantise_ctx(b * (SEQ // P) + s - 1)
+            if step + 2 < N_WINDOWS:
+                prepare_x(step + 2)
+            if step == LEAD - 1:
+                transpose_band()
+            if 0 <= step - LEAD < HALVES:
+                prepare_weight_half(wo_rows, wo_tiles, step - LEAD)

@@ -13,6 +13,7 @@ ADD = mybir.AluOpType.add
 P = 128
 PACK = 4
 BATCH, SEQ, FEATURES = 2, 512, 1024
+TOKENS = BATCH * SEQ
 TAPS, HALF = 11, 5
 TAP_SLOT = 16
 PASSES = FEATURES // (P * PACK)
@@ -20,60 +21,68 @@ BLOCKS = FEATURES // P
 N_TILE = 512
 HALVES = FEATURES // N_TILE
 
-WIN_STEP = 96
+WIN_STEP = 112
 MARGIN = (P - WIN_STEP) // 2
-WINS = (SEQ - P) // WIN_STEP + 1
-N_WINDOWS = BATCH * WINS
+N_WINDOWS = (TOKENS - P) // WIN_STEP + 1
+assert MARGIN >= HALF and (N_WINDOWS - 1) * WIN_STEP + P == TOKENS
+SEAM_WINDOW, SEAM = divmod(SEQ, WIN_STEP)
+assert (SEAM_WINDOW - 1) * WIN_STEP + P <= SEQ and SEAM == P // 2
 
 ROW_PITCH = 136
 
-LEAD = 3
-X_BEFORE_WO = LEAD + 3
+LEAD = 4
+X_BEFORE_BAND = 4
 
-FLOPS = 2 * 2 * BATCH * SEQ * FEATURES * FEATURES + 2 * BATCH * SEQ * TAPS * FEATURES
+FLOPS = 2 * 2 * TOKENS * FEATURES * FEATURES + 2 * TOKENS * TAPS * FEATURES
 
 
 def window_place(w):
-    b, s = divmod(w, WINS)
-    lo = 0 if s == 0 else MARGIN
-    hi = P if s == WINS - 1 else P - MARGIN
-    return b, s * WIN_STEP, lo, hi
+    lo = 0 if w == 0 else MARGIN
+    hi = P if w == N_WINDOWS - 1 else P - MARGIN
+    return w * WIN_STEP, lo, hi
 
 
 def tile_localattention_pb_kernel(tc, x, Wv, bv, attn_band, Wo, bo, out):
     nc = tc.nc
-    out_rows_hbm = out.rearrange("b s d -> (b s) d")
+    x_hbm = x.rearrange("b s d -> (b s) d")
+    taps_hbm = attn_band.rearrange("b s o -> (b s) o")
+    out_hbm = out.rearrange("b s d -> (b s) d")
     out_flat = out.rearrange("b s d -> (b s d)")
+    parked = out_flat[TOKENS * FEATURES - N_WINDOWS * P * ROW_PITCH : TOKENS * FEATURES]
 
     with ExitStack() as stack:
         keep = stack.enter_context(tc.tile_pool(name="keep", bufs=1))
         x_pool = stack.enter_context(tc.tile_pool(name="x_pool", bufs=N_WINDOWS))
         pairs_pool = stack.enter_context(tc.tile_pool(name="pairs_pool", bufs=3))
         v_pool = stack.enter_context(tc.tile_pool(name="v_pool", bufs=LEAD + 1))
+        ctx_pool = stack.enter_context(tc.tile_pool(name="ctx_pool", bufs=3))
         out_pool = stack.enter_context(tc.tile_pool(name="out_pool", bufs=4))
         psum = stack.enter_context(tc.psum_pool(name="psum", bufs=2))
         stack.enter_context(tc.manual_schedule())
 
-        weights_win = keep.tile([P, N_WINDOWS, TAP_SLOT], BF16)
-        for b in range(BATCH):
-            wins = slice(b * WINS, (b + 1) * WINS)
-            nc.sync.dma_start(
-                out=weights_win[0:WIN_STEP, wins, 0:TAPS],
-                in_=attn_band[b, 0 : WINS * WIN_STEP, :].rearrange("(s r) o -> r s o", r=WIN_STEP),
-            )
-            nc.sync.dma_start(
-                out=weights_win[WIN_STEP:P, wins, 0:TAPS],
-                in_=attn_band[b, P - WIN_STEP : SEQ, :].rearrange("(s r) o -> r s o", r=WIN_STEP)[
-                    2 * WIN_STEP - P : WIN_STEP
-                ],
-            )
+        ident = keep.tile([P, P], F32)
+        make_identity(nc, ident[:])
+        ident_bf = keep.tile([P, P], BF16)
+        make_identity(nc, ident_bf[:])
+
+        taps_win = keep.tile([P, N_WINDOWS, TAP_SLOT], BF16)
+        nc.sync.dma_start(
+            out=taps_win[0:WIN_STEP, :, 0:TAPS],
+            in_=taps_hbm[0 : N_WINDOWS * WIN_STEP, :].rearrange("(w r) o -> r w o", r=WIN_STEP),
+        )
+        nc.sync.dma_start(
+            out=taps_win[WIN_STEP:P, :, 0:TAPS],
+            in_=taps_hbm[P - WIN_STEP : TOKENS, :].rearrange("(w r) o -> r w o", r=WIN_STEP)[
+                2 * WIN_STEP - P : WIN_STEP
+            ],
+        )
 
         x_rows = {}
 
         def load_x(w):
-            b, first, lo, hi = window_place(w)
+            first, lo, hi = window_place(w)
             x_win = x_pool.tile([P, FEATURES], BF16)
-            nc.sync.dma_start(out=x_win[:], in_=x[b, first : first + P, :])
+            nc.sync.dma_start(out=x_win[:], in_=x_hbm[first : first + P, :])
             x_rows[w] = x_win
 
         load_x(0)
@@ -85,7 +94,26 @@ def tile_localattention_pb_kernel(tc, x, Wv, bv, attn_band, Wo, bo, out):
             )
         bv_all = keep.tile([P, FEATURES], BF16)
         nc.sync.dma_start(out=bv_all[:], in_=bv.partition_broadcast(P))
-        for w in range(1, X_BEFORE_WO):
+        for w in range(1, X_BEFORE_BAND):
+            load_x(w)
+
+        padded = keep.tile([P, N_WINDOWS, ROW_PITCH], F32)
+        nc.vector.memset(padded[:], 0.0)
+        nc.vector.tensor_copy(out=padded[:, :, 0:TAPS], in_=taps_win[:, :, 0:TAPS])
+        nc.scalar.dma_start(
+            out=parked.rearrange("(w p q) -> p w q", p=P, q=ROW_PITCH), in_=padded[:]
+        )
+        band = keep.tile([P, N_WINDOWS, P], F32)
+        nc.sync.dma_start(
+            out=band[:],
+            in_=parked.rearrange("(w r) -> w r", r=P * ROW_PITCH)[
+                :, HALF : HALF + P * (ROW_PITCH - 1)
+            ].rearrange("w (p q) -> p w q", q=ROW_PITCH - 1)[:, :, 0:P],
+        )
+        nc.gpsimd.memset(band[0:SEAM, SEAM_WINDOW, SEAM:P], 0.0)
+        nc.gpsimd.memset(band[SEAM:P, SEAM_WINDOW, 0:SEAM], 0.0)
+
+        for w in range(X_BEFORE_BAND, N_WINDOWS):
             load_x(w)
         wo_rows = keep.tile([P, BLOCKS, FEATURES], BF16)
         for q in range(BLOCKS // 2):
@@ -95,27 +123,7 @@ def tile_localattention_pb_kernel(tc, x, Wv, bv, attn_band, Wo, bo, out):
             )
         bo_all = keep.tile([P, FEATURES], BF16)
         nc.sync.dma_start(out=bo_all[:], in_=bo.partition_broadcast(P))
-        for w in range(X_BEFORE_WO, N_WINDOWS):
-            load_x(w)
 
-        ident = keep.tile([P, P], F32)
-        make_identity(nc, ident[:])
-
-        total = BATCH * SEQ * FEATURES
-        parked = out_flat[total - N_WINDOWS * P * ROW_PITCH : total]
-        padded = keep.tile([P, N_WINDOWS, ROW_PITCH], F32)
-        nc.vector.memset(padded[:], 0.0)
-        nc.vector.tensor_copy(out=padded[:, :, 0:TAPS], in_=weights_win[:, :, 0:TAPS])
-        nc.gpsimd.dma_start(
-            out=parked.rearrange("(w p q) -> p w q", p=P, q=ROW_PITCH), in_=padded[:]
-        )
-        band = keep.tile([P, N_WINDOWS, P], F32)
-        nc.gpsimd.dma_start(
-            out=band[:],
-            in_=parked.rearrange("(w r) -> w r", r=P * ROW_PITCH)[
-                :, HALF : HALF + P * (ROW_PITCH - 1)
-            ].rearrange("w (p q) -> p w q", q=ROW_PITCH - 1)[:, :, 0:P],
-        )
         band_t = keep.tile([P, N_WINDOWS, P], F32)
 
         def transpose_band():
@@ -207,28 +215,38 @@ def tile_localattention_pb_kernel(tc, x, Wv, bv, attn_band, Wo, bo, out):
                 )
             v_rows[w] = v_win
 
-        ctx_quads = keep.tile([P, PASSES, BATCH * SEQ, PACK], BF16, align_bytes=64)
-        ctx_codes = keep.tile([P, PASSES, BATCH * SEQ], U32, align_bytes=64)
-        ctx_scales = keep.tile([P, PASSES, BATCH * SEQ], U8, align_bytes=64)
+        ctx_rows = {}
 
         def mix(w):
-            b, first, lo, hi = window_place(w)
-            token = b * SEQ + first + lo
-            for c in range(PASSES):
-                mix_acc = psum.tile([P, PACK, P], F32)
-                for t in range(PACK):
-                    blk = c * PACK + t
-                    nc.tensor.matmul(
-                        out=mix_acc[:, t, 0 : hi - lo],
-                        lhsT=v_rows[w][:, blk * P : (blk + 1) * P],
-                        rhs=band_t[:, w, lo:hi],
-                        start=True,
-                        stop=True,
-                    )
-                nc.scalar.copy(
-                    out=ctx_quads[:, c, token : token + hi - lo, :],
-                    in_=mix_acc[:, :, 0 : hi - lo].rearrange("p t i -> p i t"),
+            ctx_win = ctx_pool.tile([P, FEATURES], BF16)
+            for half in range(HALVES):
+                cols = slice(half * N_TILE, (half + 1) * N_TILE)
+                mix_acc = psum.tile([P, N_TILE], F32)
+                nc.tensor.matmul(
+                    out=mix_acc[:],
+                    lhsT=band_t[:, w, :],
+                    rhs=v_rows[w][:, cols],
+                    start=True,
+                    stop=True,
                 )
+                nc.scalar.copy(out=ctx_win[:, cols], in_=mix_acc[:])
+            ctx_rows[w] = ctx_win
+
+        ctx_quads = keep.tile([P, PASSES, TOKENS, PACK], BF16, align_bytes=64)
+        ctx_codes = keep.tile([P, PASSES, TOKENS], U32, align_bytes=64)
+        ctx_scales = keep.tile([P, PASSES, TOKENS], U8, align_bytes=64)
+
+        def flip_ctx(w):
+            first, lo, hi = window_place(w)
+            flipped = psum.tile([P, BLOCKS, P], BF16, tag="flipped")
+            for blk in range(BLOCKS):
+                nc.tensor.transpose(
+                    flipped[:, blk, :], ctx_rows[w][:, blk * P : (blk + 1) * P], ident_bf[:]
+                )
+            nc.scalar.copy(
+                out=ctx_quads[:, :, first + lo : first + hi, :],
+                in_=flipped[:, :, lo:hi].rearrange("p (c t) i -> p c i t", t=PACK),
+            )
 
         def quantise_ctx(tb):
             tokens = slice(tb * P, (tb + 1) * P)
@@ -253,24 +271,24 @@ def tile_localattention_pb_kernel(tc, x, Wv, bv, attn_band, Wo, bo, out):
                 )
                 out_sb = out_pool.tile([P, N_TILE], F32)
                 nc.vector.tensor_tensor(out=out_sb[:], in0=out_acc[:], in1=bo_all[:, cols], op=ADD)
-                nc.sync.dma_start(out=out_rows_hbm[tokens, cols], in_=out_sb[:])
+                nc.sync.dma_start(out=out_hbm[tokens, cols], in_=out_sb[:])
 
         prepare_x(0)
         for half in range(HALVES):
             prepare_weight_half(wv_rows, wv_tiles, half)
         prepare_x(1)
 
-        for step in range(N_WINDOWS + LEAD + 1):
+        for step in range(N_WINDOWS + LEAD + 3):
             if step < N_WINDOWS:
                 project_v(step)
-            b, s = divmod(step - LEAD - 1, WINS)
-            if step - LEAD - 1 >= 0 and s >= 1:
-                project_out(b * (SEQ // P) + s - 1)
+            if 0 <= step - LEAD - 4 < TOKENS // P:
+                project_out(step - LEAD - 4)
             if 0 <= step - LEAD < N_WINDOWS:
                 mix(step - LEAD)
-                b, s = divmod(step - LEAD, WINS)
-                if s >= 1:
-                    quantise_ctx(b * (SEQ // P) + s - 1)
+            if 0 <= step - LEAD - 1 < N_WINDOWS:
+                flip_ctx(step - LEAD - 1)
+                if step - LEAD - 1 >= 1:
+                    quantise_ctx(step - LEAD - 2)
             if step + 2 < N_WINDOWS:
                 prepare_x(step + 2)
             if step == LEAD - 1:

@@ -17,9 +17,10 @@ TOKENS = BATCH * SEQ
 TAPS, HALF = 11, 5
 TAP_SLOT = 16
 PASSES = FEATURES // (P * PACK)
-BLOCKS = FEATURES // P
 N_TILE = 512
 HALVES = FEATURES // N_TILE
+ROW_PAIRS = FEATURES // (2 * P)
+PAIRS_PER_HALF = ROW_PAIRS // HALVES
 
 WIN_STEP = 112
 MARGIN = (P - WIN_STEP) // 2
@@ -30,8 +31,7 @@ assert (SEAM_WINDOW - 1) * WIN_STEP + P <= SEQ and SEAM == P // 2
 
 ROW_PITCH = 136
 
-LEAD = 4
-X_BEFORE_BAND = 4
+ROUND = 2
 
 FLOPS = 2 * 2 * TOKENS * FEATURES * FEATURES + 2 * TOKENS * TAPS * FEATURES
 
@@ -54,10 +54,10 @@ def tile_localattention_pb_kernel(tc, x, Wv, bv, attn_band, Wo, bo, out):
         keep = stack.enter_context(tc.tile_pool(name="keep", bufs=1))
         x_pool = stack.enter_context(tc.tile_pool(name="x_pool", bufs=N_WINDOWS))
         pairs_pool = stack.enter_context(tc.tile_pool(name="pairs_pool", bufs=3))
-        v_pool = stack.enter_context(tc.tile_pool(name="v_pool", bufs=LEAD + 1))
+        v_pool = stack.enter_context(tc.tile_pool(name="v_pool", bufs=N_WINDOWS))
         ctx_pool = stack.enter_context(tc.tile_pool(name="ctx_pool", bufs=3))
         out_pool = stack.enter_context(tc.tile_pool(name="out_pool", bufs=4))
-        psum = stack.enter_context(tc.psum_pool(name="psum", bufs=2))
+        psum = stack.enter_context(tc.psum_pool(name="psum", bufs=4))
         stack.enter_context(tc.manual_schedule())
 
         ident = keep.tile([P, P], F32)
@@ -65,16 +65,32 @@ def tile_localattention_pb_kernel(tc, x, Wv, bv, attn_band, Wo, bo, out):
         ident_bf = keep.tile([P, P], BF16)
         make_identity(nc, ident_bf[:])
 
+        ones = keep.tile([P, P], BF16)
+        nc.vector.memset(ones[:], 1.0)
+        bias_rows = {}
+        for label, bias in (("bv", bv), ("bo", bo)):
+            bias_row = keep.tile([P, FEATURES], BF16, name=label + "_row")
+            nc.vector.memset(bias_row[:], 0.0)
+            nc.scalar.dma_start(out=bias_row[0:1, :], in_=bias.rearrange("(o n) -> o n", o=1))
+            bias_rows[label] = bias_row
+
         taps_win = keep.tile([P, N_WINDOWS, TAP_SLOT], BF16)
-        nc.sync.dma_start(
+        nc.scalar.dma_start(
             out=taps_win[0:WIN_STEP, :, 0:TAPS],
             in_=taps_hbm[0 : N_WINDOWS * WIN_STEP, :].rearrange("(w r) o -> r w o", r=WIN_STEP),
         )
-        nc.sync.dma_start(
+        nc.scalar.dma_start(
             out=taps_win[WIN_STEP:P, :, 0:TAPS],
             in_=taps_hbm[P - WIN_STEP : TOKENS, :].rearrange("(w r) o -> r w o", r=WIN_STEP)[
                 2 * WIN_STEP - P : WIN_STEP
             ],
+        )
+
+        padded = keep.tile([P, N_WINDOWS, ROW_PITCH], F32)
+        nc.vector.memset(padded[:], 0.0)
+        nc.vector.tensor_copy(out=padded[:, :, 0:TAPS], in_=taps_win[:, :, 0:TAPS])
+        nc.gpsimd.dma_start(
+            out=parked.rearrange("(w p q) -> p w q", p=P, q=ROW_PITCH), in_=padded[:]
         )
 
         x_rows = {}
@@ -86,23 +102,15 @@ def tile_localattention_pb_kernel(tc, x, Wv, bv, attn_band, Wo, bo, out):
             x_rows[w] = x_win
 
         load_x(0)
-        wv_rows = keep.tile([P, BLOCKS, FEATURES], BF16)
-        for q in range(BLOCKS // 2):
+        wv_rows = keep.tile([P, ROW_PAIRS, 2, FEATURES], BF16)
+        for q in range(ROW_PAIRS):
             nc.sync.dma_start(
-                out=wv_rows[:, 2 * q : 2 * q + 2, :],
+                out=wv_rows[:, q, :, :],
                 in_=Wv[2 * P * q : 2 * P * (q + 1), :].rearrange("(m e) k -> m e k", e=2),
             )
-        bv_all = keep.tile([P, FEATURES], BF16)
-        nc.sync.dma_start(out=bv_all[:], in_=bv.partition_broadcast(P))
-        for w in range(1, X_BEFORE_BAND):
+        for w in range(1, N_WINDOWS):
             load_x(w)
 
-        padded = keep.tile([P, N_WINDOWS, ROW_PITCH], F32)
-        nc.vector.memset(padded[:], 0.0)
-        nc.vector.tensor_copy(out=padded[:, :, 0:TAPS], in_=taps_win[:, :, 0:TAPS])
-        nc.scalar.dma_start(
-            out=parked.rearrange("(w p q) -> p w q", p=P, q=ROW_PITCH), in_=padded[:]
-        )
         band = keep.tile([P, N_WINDOWS, P], F32)
         nc.sync.dma_start(
             out=band[:],
@@ -113,16 +121,12 @@ def tile_localattention_pb_kernel(tc, x, Wv, bv, attn_band, Wo, bo, out):
         nc.gpsimd.memset(band[0:SEAM, SEAM_WINDOW, SEAM:P], 0.0)
         nc.gpsimd.memset(band[SEAM:P, SEAM_WINDOW, 0:SEAM], 0.0)
 
-        for w in range(X_BEFORE_BAND, N_WINDOWS):
-            load_x(w)
-        wo_rows = keep.tile([P, BLOCKS, FEATURES], BF16)
-        for q in range(BLOCKS // 2):
+        wo_rows = keep.tile([P, ROW_PAIRS, 2, FEATURES], BF16)
+        for q in range(ROW_PAIRS):
             nc.sync.dma_start(
-                out=wo_rows[:, 2 * q : 2 * q + 2, :],
+                out=wo_rows[:, q, :, :],
                 in_=Wo[2 * P * q : 2 * P * (q + 1), :].rearrange("(j m) k -> m j k", m=P),
             )
-        bo_all = keep.tile([P, FEATURES], BF16)
-        nc.sync.dma_start(out=bo_all[:], in_=bo.partition_broadcast(P))
 
         band_t = keep.tile([P, N_WINDOWS, P], F32)
 
@@ -145,42 +149,37 @@ def tile_localattention_pb_kernel(tc, x, Wv, bv, attn_band, Wo, bo, out):
         x_scales = keep.tile([P, N_WINDOWS, PASSES, P], U8, align_bytes=64)
 
         def prepare_x(w):
-            x_pairs = pairs_pool.tile([P, PASSES * P * 2], F32, align_bytes=64)
-            transpose_rows(
-                x_rows[w][:],
-                x_pairs[:].rearrange("p (c r u) -> p c r u", c=PASSES, u=2),
-                nc.scalar.copy,
-            )
+            x_pairs = pairs_pool.tile([P, PASSES, P, 2], F32, align_bytes=64)
+            transpose_rows(x_rows[w][:], x_pairs[:], nc.scalar.copy)
             nc.vector.quantize_mx(
                 out=x_codes[:, w, :, :].rearrange("p c r -> p (c r)").bitcast(FP8X4),
                 scales=x_scales[:, w, :, :].rearrange("p c r -> p (c r)"),
-                in_=x_pairs[:].bitcast(BF16),
+                in_=x_pairs[:].rearrange("p c r u -> p (c r u)").bitcast(BF16),
             )
 
         def weight_tiles(label):
-            pairs = keep.tile([P, PASSES, FEATURES, 2], F32, name=label + "_pairs", align_bytes=64)
             codes = keep.tile([P, PASSES, FEATURES], U32, name=label + "_codes", align_bytes=64)
             scales = keep.tile([P, PASSES, FEATURES], U8, name=label + "_scales", align_bytes=64)
-            return pairs, codes, scales
+            return codes, scales
 
-        def prepare_weight_half(rows, tiles, half):
-            pairs, codes, scales = tiles
-            for blk in range(half * PACK, (half + 1) * PACK):
-                copy = nc.scalar.copy if blk % 2 == 0 else nc.vector.tensor_copy
-                transpose_rows(rows[:, blk, :], pairs[:, :, blk * P : (blk + 1) * P, :], copy)
-            cols = slice(half * N_TILE, (half + 1) * N_TILE)
+        def prepare_weight_pair(rows, tiles, q):
+            codes, scales = tiles
+            w_pairs = pairs_pool.tile([P, PASSES, 2 * P, 2], F32, align_bytes=64)
+            transpose_rows(rows[:, q, 0, :], w_pairs[:, :, 0:P, :], nc.scalar.copy)
+            transpose_rows(rows[:, q, 1, :], w_pairs[:, :, P : 2 * P, :], nc.vector.tensor_copy)
+            cols = slice(2 * P * q, 2 * P * (q + 1))
             for c in range(PASSES):
                 nc.vector.quantize_mx(
                     out=codes[:, c, cols].bitcast(FP8X4),
                     scales=scales[:, c, cols],
-                    in_=pairs[:, c, cols, :].rearrange("p n u -> p (n u)").bitcast(BF16),
+                    in_=w_pairs[:, c, :, :].rearrange("p n u -> p (n u)").bitcast(BF16),
                 )
 
         wv_tiles = weight_tiles("wv")
         wo_tiles = weight_tiles("wo")
 
         def product(acc, left_codes, left_scales, tiles, half):
-            pairs, codes, scales = tiles
+            codes, scales = tiles
             cols = slice(half * N_TILE, (half + 1) * N_TILE)
             for c in range(PASSES):
                 nc.tensor.matmul_mx(
@@ -193,13 +192,33 @@ def tile_localattention_pb_kernel(tc, x, Wv, bv, attn_band, Wo, bo, out):
                     stop=(c == PASSES - 1),
                 )
 
+        bv_all = keep.tile([P, FEATURES], F32)
+        bo_all = keep.tile([P, FEATURES], F32)
+
+        def spread_biases():
+            for half in range(HALVES):
+                cols = slice(half * N_TILE, (half + 1) * N_TILE)
+                bv_acc = psum.tile([P, N_TILE], F32, tag="acc")
+                nc.tensor.matmul(
+                    out=bv_acc[:], lhsT=ones[:], rhs=bias_rows["bv"][:, cols], start=True, stop=True
+                )
+                nc.scalar.copy(
+                    out=bv_all[:, cols].rearrange("p (u e m) -> p u e m", u=2, e=2),
+                    in_=bv_acc[:].rearrange("p (u m e) -> p u e m", u=2, e=2),
+                )
+                bo_acc = psum.tile([P, N_TILE], F32, tag="acc")
+                nc.tensor.matmul(
+                    out=bo_acc[:], lhsT=ones[:], rhs=bias_rows["bo"][:, cols], start=True, stop=True
+                )
+                nc.scalar.copy(out=bo_all[:, cols], in_=bo_acc[:])
+
         v_rows = {}
 
         def project_v(w):
             v_win = v_pool.tile([P, FEATURES], F32)
             for half in range(HALVES):
                 cols = slice(half * N_TILE, (half + 1) * N_TILE)
-                v_acc = psum.tile([P, N_TILE], F32)
+                v_acc = psum.tile([P, N_TILE], F32, tag="acc")
                 product(
                     v_acc[:],
                     [x_codes[:, w, c, :] for c in range(PASSES)],
@@ -208,10 +227,7 @@ def tile_localattention_pb_kernel(tc, x, Wv, bv, attn_band, Wo, bo, out):
                     half,
                 )
                 nc.vector.tensor_tensor(
-                    out=v_win[:, cols].rearrange("p (u e m) -> p u e m", u=2, e=2),
-                    in0=v_acc[:].rearrange("p (u e m) -> p u e m", u=2, e=2),
-                    in1=bv_all[:, cols].rearrange("p (u m e) -> p u e m", u=2, e=2),
-                    op=ADD,
+                    out=v_win[:, cols], in0=v_acc[:], in1=bv_all[:, cols], op=ADD
                 )
             v_rows[w] = v_win
 
@@ -221,7 +237,7 @@ def tile_localattention_pb_kernel(tc, x, Wv, bv, attn_band, Wo, bo, out):
             ctx_win = ctx_pool.tile([P, FEATURES], BF16)
             for half in range(HALVES):
                 cols = slice(half * N_TILE, (half + 1) * N_TILE)
-                mix_acc = psum.tile([P, N_TILE], F32)
+                mix_acc = psum.tile([P, N_TILE], F32, tag="acc")
                 nc.tensor.matmul(
                     out=mix_acc[:],
                     lhsT=band_t[:, w, :],
@@ -238,15 +254,18 @@ def tile_localattention_pb_kernel(tc, x, Wv, bv, attn_band, Wo, bo, out):
 
         def flip_ctx(w):
             first, lo, hi = window_place(w)
-            flipped = psum.tile([P, BLOCKS, P], BF16, tag="flipped")
-            for blk in range(BLOCKS):
-                nc.tensor.transpose(
-                    flipped[:, blk, :], ctx_rows[w][:, blk * P : (blk + 1) * P], ident_bf[:]
+            for c in range(PASSES):
+                flipped = psum.tile([P, PACK, P], BF16, tag="flipped")
+                for t in range(PACK):
+                    blk = c * PACK + t
+                    nc.tensor.transpose(
+                        flipped[:, t, :], ctx_rows[w][:, blk * P : (blk + 1) * P], ident_bf[:]
+                    )
+                copy = nc.scalar.copy if c == 0 else nc.vector.tensor_copy
+                copy(
+                    out=ctx_quads[:, c, first + lo : first + hi, :],
+                    in_=flipped[:, :, lo:hi].rearrange("p t i -> p i t"),
                 )
-            nc.scalar.copy(
-                out=ctx_quads[:, :, first + lo : first + hi, :],
-                in_=flipped[:, :, lo:hi].rearrange("p (c t) i -> p c i t", t=PACK),
-            )
 
         def quantise_ctx(tb):
             tokens = slice(tb * P, (tb + 1) * P)
@@ -261,7 +280,7 @@ def tile_localattention_pb_kernel(tc, x, Wv, bv, attn_band, Wo, bo, out):
             tokens = slice(tb * P, (tb + 1) * P)
             for half in range(HALVES):
                 cols = slice(half * N_TILE, (half + 1) * N_TILE)
-                out_acc = psum.tile([P, N_TILE], F32)
+                out_acc = psum.tile([P, N_TILE], F32, tag="acc")
                 product(
                     out_acc[:],
                     [ctx_codes[:, c, tokens] for c in range(PASSES)],
@@ -274,24 +293,28 @@ def tile_localattention_pb_kernel(tc, x, Wv, bv, attn_band, Wo, bo, out):
                 nc.sync.dma_start(out=out_hbm[tokens, cols], in_=out_sb[:])
 
         prepare_x(0)
-        for half in range(HALVES):
-            prepare_weight_half(wv_rows, wv_tiles, half)
-        prepare_x(1)
-
-        for step in range(N_WINDOWS + LEAD + 3):
-            if step < N_WINDOWS:
-                project_v(step)
-            if 0 <= step - LEAD - 4 < TOKENS // P:
-                project_out(step - LEAD - 4)
-            if 0 <= step - LEAD < N_WINDOWS:
-                mix(step - LEAD)
-            if 0 <= step - LEAD - 1 < N_WINDOWS:
-                flip_ctx(step - LEAD - 1)
-                if step - LEAD - 1 >= 1:
-                    quantise_ctx(step - LEAD - 2)
-            if step + 2 < N_WINDOWS:
-                prepare_x(step + 2)
-            if step == LEAD - 1:
+        spread_biases()
+        for q in range(ROW_PAIRS):
+            prepare_weight_pair(wv_rows, wv_tiles, q)
+        for w in range(1, ROUND):
+            prepare_x(w)
+        for first_w in range(0, N_WINDOWS, ROUND):
+            for w in range(first_w + ROUND, min(first_w + 2 * ROUND, N_WINDOWS)):
+                prepare_x(w)
+            if first_w + ROUND >= N_WINDOWS:
                 transpose_band()
-            if 0 <= step - LEAD < HALVES:
-                prepare_weight_half(wo_rows, wo_tiles, step - LEAD)
+            for w in range(first_w, min(first_w + ROUND, N_WINDOWS)):
+                project_v(w)
+
+        for w in range(N_WINDOWS + 1):
+            if w < N_WINDOWS:
+                mix(w)
+            if w >= 2:
+                project_out(w - 2)
+            if w < HALVES:
+                for q in range(w * PAIRS_PER_HALF, (w + 1) * PAIRS_PER_HALF):
+                    prepare_weight_pair(wo_rows, wo_tiles, q)
+            if w < N_WINDOWS:
+                flip_ctx(w)
+            if 1 <= w < N_WINDOWS:
+                quantise_ctx(w - 1)

@@ -54,7 +54,7 @@ def tile_localattention_pb_kernel(tc, x, Wv, bv, attn_band, Wo, bo, out):
         keep = stack.enter_context(tc.tile_pool(name="keep", bufs=1))
         x_pool = stack.enter_context(tc.tile_pool(name="x_pool", bufs=N_WINDOWS))
         pairs_pool = stack.enter_context(tc.tile_pool(name="pairs_pool", bufs=3))
-        v_pool = stack.enter_context(tc.tile_pool(name="v_pool", bufs=N_WINDOWS))
+        v_pool = stack.enter_context(tc.tile_pool(name="v_pool", bufs=N_WINDOWS * HALVES))
         ctx_pool = stack.enter_context(tc.tile_pool(name="ctx_pool", bufs=3))
         out_pool = stack.enter_context(tc.tile_pool(name="out_pool", bufs=4))
         psum = stack.enter_context(tc.psum_pool(name="psum", bufs=4))
@@ -62,8 +62,6 @@ def tile_localattention_pb_kernel(tc, x, Wv, bv, attn_band, Wo, bo, out):
 
         ident = keep.tile([P, P], F32)
         make_identity(nc, ident[:])
-        ident_bf = keep.tile([P, P], BF16)
-        make_identity(nc, ident_bf[:])
 
         ones = keep.tile([P, P], BF16)
         nc.vector.memset(ones[:], 1.0)
@@ -86,6 +84,9 @@ def tile_localattention_pb_kernel(tc, x, Wv, bv, attn_band, Wo, bo, out):
             ],
         )
 
+        ident_bf = keep.tile([P, P], BF16)
+        nc.scalar.copy(out=ident_bf[:], in_=ident[:])
+
         padded = keep.tile([P, N_WINDOWS, ROW_PITCH], F32)
         nc.vector.memset(padded[:], 0.0)
         nc.vector.tensor_copy(out=padded[:, :, 0:TAPS], in_=taps_win[:, :, 0:TAPS])
@@ -101,13 +102,17 @@ def tile_localattention_pb_kernel(tc, x, Wv, bv, attn_band, Wo, bo, out):
             nc.sync.dma_start(out=x_win[:], in_=x_hbm[first : first + P, :])
             x_rows[w] = x_win
 
-        load_x(0)
         wv_rows = keep.tile([P, ROW_PAIRS, 2, FEATURES], BF16)
-        for q in range(ROW_PAIRS):
-            nc.sync.dma_start(
-                out=wv_rows[:, q, :, :],
-                in_=Wv[2 * P * q : 2 * P * (q + 1), :].rearrange("(m e) k -> m e k", e=2),
-            )
+
+        def load_wv_half(half):
+            for q in range(half * PAIRS_PER_HALF, (half + 1) * PAIRS_PER_HALF):
+                nc.sync.dma_start(
+                    out=wv_rows[:, q, :, :],
+                    in_=Wv[2 * P * q : 2 * P * (q + 1), :].rearrange("(m e) k -> m e k", e=2),
+                )
+
+        load_x(0)
+        load_wv_half(0)
         for w in range(1, N_WINDOWS):
             load_x(w)
 
@@ -121,6 +126,7 @@ def tile_localattention_pb_kernel(tc, x, Wv, bv, attn_band, Wo, bo, out):
         nc.gpsimd.memset(band[0:SEAM, SEAM_WINDOW, SEAM:P], 0.0)
         nc.gpsimd.memset(band[SEAM:P, SEAM_WINDOW, 0:SEAM], 0.0)
 
+        load_wv_half(1)
         wo_rows = keep.tile([P, ROW_PAIRS, 2, FEATURES], BF16)
         for q in range(ROW_PAIRS):
             nc.sync.dma_start(
@@ -175,6 +181,10 @@ def tile_localattention_pb_kernel(tc, x, Wv, bv, attn_band, Wo, bo, out):
                     in_=w_pairs[:, c, :, :].rearrange("p n u -> p (n u)").bitcast(BF16),
                 )
 
+        def prepare_weight_half(rows, tiles, half):
+            for q in range(half * PAIRS_PER_HALF, (half + 1) * PAIRS_PER_HALF):
+                prepare_weight_pair(rows, tiles, q)
+
         wv_tiles = weight_tiles("wv")
         wo_tiles = weight_tiles("wo")
 
@@ -210,26 +220,23 @@ def tile_localattention_pb_kernel(tc, x, Wv, bv, attn_band, Wo, bo, out):
                 nc.tensor.matmul(
                     out=bo_acc[:], lhsT=ones[:], rhs=bias_rows["bo"][:, cols], start=True, stop=True
                 )
-                nc.scalar.copy(out=bo_all[:, cols], in_=bo_acc[:])
+                nc.vector.tensor_copy(out=bo_all[:, cols], in_=bo_acc[:])
 
         v_rows = {}
 
-        def project_v(w):
-            v_win = v_pool.tile([P, FEATURES], F32)
-            for half in range(HALVES):
-                cols = slice(half * N_TILE, (half + 1) * N_TILE)
-                v_acc = psum.tile([P, N_TILE], F32, tag="acc")
-                product(
-                    v_acc[:],
-                    [x_codes[:, w, c, :] for c in range(PASSES)],
-                    [x_scales[:, w, c, :] for c in range(PASSES)],
-                    wv_tiles,
-                    half,
-                )
-                nc.vector.tensor_tensor(
-                    out=v_win[:, cols], in0=v_acc[:], in1=bv_all[:, cols], op=ADD
-                )
-            v_rows[w] = v_win
+        def project_v(w, half):
+            cols = slice(half * N_TILE, (half + 1) * N_TILE)
+            v_acc = psum.tile([P, N_TILE], F32, tag="acc")
+            product(
+                v_acc[:],
+                [x_codes[:, w, c, :] for c in range(PASSES)],
+                [x_scales[:, w, c, :] for c in range(PASSES)],
+                wv_tiles,
+                half,
+            )
+            v_half = v_pool.tile([P, N_TILE], F32)
+            nc.vector.tensor_tensor(out=v_half[:], in0=v_acc[:], in1=bv_all[:, cols], op=ADD)
+            v_rows[w, half] = v_half
 
         ctx_rows = {}
 
@@ -241,7 +248,7 @@ def tile_localattention_pb_kernel(tc, x, Wv, bv, attn_band, Wo, bo, out):
                 nc.tensor.matmul(
                     out=mix_acc[:],
                     lhsT=band_t[:, w, :],
-                    rhs=v_rows[w][:, cols],
+                    rhs=v_rows[w, half][:],
                     start=True,
                     stop=True,
                 )
@@ -294,17 +301,19 @@ def tile_localattention_pb_kernel(tc, x, Wv, bv, attn_band, Wo, bo, out):
 
         prepare_x(0)
         spread_biases()
-        for q in range(ROW_PAIRS):
-            prepare_weight_pair(wv_rows, wv_tiles, q)
+        prepare_weight_half(wv_rows, wv_tiles, 0)
         for w in range(1, ROUND):
             prepare_x(w)
         for first_w in range(0, N_WINDOWS, ROUND):
             for w in range(first_w + ROUND, min(first_w + 2 * ROUND, N_WINDOWS)):
                 prepare_x(w)
             if first_w + ROUND >= N_WINDOWS:
+                prepare_weight_half(wv_rows, wv_tiles, 1)
                 transpose_band()
             for w in range(first_w, min(first_w + ROUND, N_WINDOWS)):
-                project_v(w)
+                project_v(w, 0)
+        for w in range(N_WINDOWS):
+            project_v(w, 1)
 
         for w in range(N_WINDOWS + 1):
             if w < N_WINDOWS:
@@ -312,8 +321,7 @@ def tile_localattention_pb_kernel(tc, x, Wv, bv, attn_band, Wo, bo, out):
             if w >= 2:
                 project_out(w - 2)
             if w < HALVES:
-                for q in range(w * PAIRS_PER_HALF, (w + 1) * PAIRS_PER_HALF):
-                    prepare_weight_pair(wo_rows, wo_tiles, q)
+                prepare_weight_half(wo_rows, wo_tiles, w)
             if w < N_WINDOWS:
                 flip_ctx(w)
             if 1 <= w < N_WINDOWS:

@@ -9,6 +9,7 @@ U32 = mybir.dt.uint32
 U8 = mybir.dt.uint8
 FP8X4 = mybir.dt.float8_e4m3fn_x4
 ADD = mybir.AluOpType.add
+MULT = mybir.AluOpType.mult
 
 P = 128
 PACK = 4
@@ -54,7 +55,7 @@ def tile_localattention_pb_kernel(tc, x, Wv, bv, attn_band, Wo, bo, out):
         keep = stack.enter_context(tc.tile_pool(name="keep", bufs=1))
         x_pool = stack.enter_context(tc.tile_pool(name="x_pool", bufs=N_WINDOWS))
         pairs_pool = stack.enter_context(tc.tile_pool(name="pairs_pool", bufs=3))
-        v_pool = stack.enter_context(tc.tile_pool(name="v_pool", bufs=N_WINDOWS * HALVES))
+        xw_pool = stack.enter_context(tc.tile_pool(name="xw_pool", bufs=N_WINDOWS * HALVES))
         ctx_pool = stack.enter_context(tc.tile_pool(name="ctx_pool", bufs=3))
         out_pool = stack.enter_context(tc.tile_pool(name="out_pool", bufs=4))
         psum = stack.enter_context(tc.psum_pool(name="psum", bufs=4))
@@ -135,8 +136,12 @@ def tile_localattention_pb_kernel(tc, x, Wv, bv, attn_band, Wo, bo, out):
             )
 
         band_t = keep.tile([P, N_WINDOWS, P], F32)
+        tap_sums = keep.tile([P, N_WINDOWS], F32)
 
-        def transpose_band():
+        def prepare_band():
+            nc.vector.tensor_reduce(
+                out=tap_sums[:], in_=band[:], axis=mybir.AxisListType.X, op=ADD
+            )
             for w0 in range(0, N_WINDOWS, PACK):
                 count = min(PACK, N_WINDOWS - w0)
                 flipped = psum.tile([P, PACK, P], F32, tag="flipped")
@@ -222,21 +227,21 @@ def tile_localattention_pb_kernel(tc, x, Wv, bv, attn_band, Wo, bo, out):
                 )
                 nc.vector.tensor_copy(out=bo_all[:, cols], in_=bo_acc[:])
 
-        v_rows = {}
+        xw_rows = {}
 
-        def project_v(w, half):
-            cols = slice(half * N_TILE, (half + 1) * N_TILE)
-            v_acc = psum.tile([P, N_TILE], F32, tag="acc")
+        def project_xw(w, half):
+            xw_acc = psum.tile([P, N_TILE], F32, tag="acc")
             product(
-                v_acc[:],
+                xw_acc[:],
                 [x_codes[:, w, c, :] for c in range(PASSES)],
                 [x_scales[:, w, c, :] for c in range(PASSES)],
                 wv_tiles,
                 half,
             )
-            v_half = v_pool.tile([P, N_TILE], F32)
-            nc.vector.tensor_tensor(out=v_half[:], in0=v_acc[:], in1=bv_all[:, cols], op=ADD)
-            v_rows[w, half] = v_half
+            xw_half = xw_pool.tile([P, N_TILE], F32)
+            copy = nc.scalar.copy if w % 2 == 0 else nc.vector.tensor_copy
+            copy(out=xw_half[:], in_=xw_acc[:])
+            xw_rows[w, half] = xw_half
 
         ctx_rows = {}
 
@@ -248,11 +253,18 @@ def tile_localattention_pb_kernel(tc, x, Wv, bv, attn_band, Wo, bo, out):
                 nc.tensor.matmul(
                     out=mix_acc[:],
                     lhsT=band_t[:, w, :],
-                    rhs=v_rows[w, half][:],
+                    rhs=xw_rows[w, half][:],
                     start=True,
                     stop=True,
                 )
-                nc.scalar.copy(out=ctx_win[:, cols], in_=mix_acc[:])
+                nc.vector.scalar_tensor_tensor(
+                    out=ctx_win[:, cols],
+                    in0=bv_all[:, cols],
+                    scalar=tap_sums[:, w : w + 1],
+                    in1=mix_acc[:],
+                    op0=MULT,
+                    op1=ADD,
+                )
             ctx_rows[w] = ctx_win
 
         ctx_quads = keep.tile([P, PASSES, TOKENS, PACK], BF16, align_bytes=64)
@@ -268,8 +280,7 @@ def tile_localattention_pb_kernel(tc, x, Wv, bv, attn_band, Wo, bo, out):
                     nc.tensor.transpose(
                         flipped[:, t, :], ctx_rows[w][:, blk * P : (blk + 1) * P], ident_bf[:]
                     )
-                copy = nc.scalar.copy if c == 0 else nc.vector.tensor_copy
-                copy(
+                nc.scalar.copy(
                     out=ctx_quads[:, c, first + lo : first + hi, :],
                     in_=flipped[:, :, lo:hi].rearrange("p t i -> p i t"),
                 )
@@ -309,11 +320,11 @@ def tile_localattention_pb_kernel(tc, x, Wv, bv, attn_band, Wo, bo, out):
                 prepare_x(w)
             if first_w + ROUND >= N_WINDOWS:
                 prepare_weight_half(wv_rows, wv_tiles, 1)
-                transpose_band()
+                prepare_band()
             for w in range(first_w, min(first_w + ROUND, N_WINDOWS)):
-                project_v(w, 0)
+                project_xw(w, 0)
         for w in range(N_WINDOWS):
-            project_v(w, 1)
+            project_xw(w, 1)
 
         for w in range(N_WINDOWS + 1):
             if w < N_WINDOWS:

from contextlib import ExitStack

import concourse.mybir as mybir
from concourse.masks import make_identity

F32 = mybir.dt.float32
BF16 = mybir.dt.bfloat16
U32 = mybir.dt.uint32
U8 = mybir.dt.uint8
FP8X4 = mybir.dt.float8_e4m3fn_x4
ADD = mybir.AluOpType.add
MULT = mybir.AluOpType.mult

P = 128
PACK = 4
BATCH, SEQ, FEATURES = 2, 512, 1024
TOKENS = BATCH * SEQ
TAPS, HALF = 11, 5
TAP_SLOT = 16
PASSES = FEATURES // (P * PACK)
N_TILE = 512
HALVES = FEATURES // N_TILE
ROW_PAIRS = FEATURES // (2 * P)
PAIRS_PER_HALF = ROW_PAIRS // HALVES

WIN_STEP = 112
MARGIN = (P - WIN_STEP) // 2
N_WINDOWS = (TOKENS - P) // WIN_STEP + 1
assert MARGIN >= HALF and (N_WINDOWS - 1) * WIN_STEP + P == TOKENS
SEAM_WINDOW, SEAM = divmod(SEQ, WIN_STEP)
assert (SEAM_WINDOW - 1) * WIN_STEP + P <= SEQ and SEAM == P // 2

ROW_PITCH = 136

ROUND = 2

FLOPS = 2 * 2 * TOKENS * FEATURES * FEATURES + 2 * TOKENS * TAPS * FEATURES


def window_place(w):
    lo = 0 if w == 0 else MARGIN
    hi = P if w == N_WINDOWS - 1 else P - MARGIN
    return w * WIN_STEP, lo, hi


def tile_localattention_pb_kernel(tc, x, Wv, bv, attn_band, Wo, bo, out):
    nc = tc.nc
    x_hbm = x.rearrange("b s d -> (b s) d")
    taps_hbm = attn_band.rearrange("b s o -> (b s) o")
    out_hbm = out.rearrange("b s d -> (b s) d")
    out_flat = out.rearrange("b s d -> (b s d)")
    parked = out_flat[TOKENS * FEATURES - N_WINDOWS * P * ROW_PITCH : TOKENS * FEATURES]

    with ExitStack() as stack:
        keep = stack.enter_context(tc.tile_pool(name="keep", bufs=1))
        x_pool = stack.enter_context(tc.tile_pool(name="x_pool", bufs=N_WINDOWS))
        pairs_pool = stack.enter_context(tc.tile_pool(name="pairs_pool", bufs=3))
        xw_pool = stack.enter_context(tc.tile_pool(name="xw_pool", bufs=N_WINDOWS * HALVES))
        ctx_pool = stack.enter_context(tc.tile_pool(name="ctx_pool", bufs=3))
        out_pool = stack.enter_context(tc.tile_pool(name="out_pool", bufs=4))
        psum = stack.enter_context(tc.psum_pool(name="psum", bufs=4))
        stack.enter_context(tc.manual_schedule())

        ident = keep.tile([P, P], F32)
        make_identity(nc, ident[:])

        ones = keep.tile([P, P], BF16)
        nc.vector.memset(ones[:], 1.0)
        bias_rows = {}
        for label, bias in (("bv", bv), ("bo", bo)):
            bias_row = keep.tile([P, FEATURES], BF16, name=label + "_row")
            nc.vector.memset(bias_row[:], 0.0)
            nc.scalar.dma_start(out=bias_row[0:1, :], in_=bias.rearrange("(o n) -> o n", o=1))
            bias_rows[label] = bias_row

        taps_win = keep.tile([P, N_WINDOWS, TAP_SLOT], BF16)
        nc.scalar.dma_start(
            out=taps_win[0:WIN_STEP, :, 0:TAPS],
            in_=taps_hbm[0 : N_WINDOWS * WIN_STEP, :].rearrange("(w r) o -> r w o", r=WIN_STEP),
        )
        nc.scalar.dma_start(
            out=taps_win[WIN_STEP:P, :, 0:TAPS],
            in_=taps_hbm[P - WIN_STEP : TOKENS, :].rearrange("(w r) o -> r w o", r=WIN_STEP)[
                2 * WIN_STEP - P : WIN_STEP
            ],
        )

        ident_bf = keep.tile([P, P], BF16)
        nc.scalar.copy(out=ident_bf[:], in_=ident[:])

        padded = keep.tile([P, N_WINDOWS, ROW_PITCH], F32)
        nc.vector.memset(padded[:], 0.0)
        nc.vector.tensor_copy(out=padded[:, :, 0:TAPS], in_=taps_win[:, :, 0:TAPS])
        nc.gpsimd.dma_start(
            out=parked.rearrange("(w p q) -> p w q", p=P, q=ROW_PITCH), in_=padded[:]
        )

        x_rows = {}

        def load_x(w):
            first, lo, hi = window_place(w)
            x_win = x_pool.tile([P, FEATURES], BF16)
            nc.sync.dma_start(out=x_win[:], in_=x_hbm[first : first + P, :])
            x_rows[w] = x_win

        wv_rows = keep.tile([P, ROW_PAIRS, 2, FEATURES], BF16)

        def load_wv_half(half):
            for q in range(half * PAIRS_PER_HALF, (half + 1) * PAIRS_PER_HALF):
                nc.sync.dma_start(
                    out=wv_rows[:, q, :, :],
                    in_=Wv[2 * P * q : 2 * P * (q + 1), :].rearrange("(m e) k -> m e k", e=2),
                )

        load_x(0)
        load_wv_half(0)
        for w in range(1, N_WINDOWS):
            load_x(w)

        band = keep.tile([P, N_WINDOWS, P], F32)
        nc.sync.dma_start(
            out=band[:],
            in_=parked.rearrange("(w r) -> w r", r=P * ROW_PITCH)[
                :, HALF : HALF + P * (ROW_PITCH - 1)
            ].rearrange("w (p q) -> p w q", q=ROW_PITCH - 1)[:, :, 0:P],
        )
        nc.gpsimd.memset(band[0:SEAM, SEAM_WINDOW, SEAM:P], 0.0)
        nc.gpsimd.memset(band[SEAM:P, SEAM_WINDOW, 0:SEAM], 0.0)

        load_wv_half(1)
        wo_rows = keep.tile([P, ROW_PAIRS, 2, FEATURES], BF16)
        for q in range(ROW_PAIRS):
            nc.sync.dma_start(
                out=wo_rows[:, q, :, :],
                in_=Wo[2 * P * q : 2 * P * (q + 1), :].rearrange("(j m) k -> m j k", m=P),
            )

        band_t = keep.tile([P, N_WINDOWS, P], F32)
        tap_sums = keep.tile([P, N_WINDOWS], F32)

        def prepare_band():
            nc.vector.tensor_reduce(
                out=tap_sums[:], in_=band[:], axis=mybir.AxisListType.X, op=ADD
            )
            for w0 in range(0, N_WINDOWS, PACK):
                count = min(PACK, N_WINDOWS - w0)
                flipped = psum.tile([P, PACK, P], F32, tag="flipped")
                for j in range(count):
                    nc.tensor.transpose(flipped[:, j, :], band[:, w0 + j, :], ident[:])
                nc.scalar.copy(out=band_t[:, w0 : w0 + count, :], in_=flipped[:, 0:count, :])

        def transpose_rows(rows, pairs, copy):
            words = rows.bitcast(F32)
            flipped = psum.tile([P, PACK, P], F32, tag="flipped")
            for j in range(PACK):
                nc.tensor.transpose(flipped[:, j, :], words[:, j * P : (j + 1) * P], ident[:])
            copy(out=pairs, in_=flipped[:].rearrange("p (c u) r -> p c r u", u=2))

        x_codes = keep.tile([P, N_WINDOWS, PASSES, P], U32, align_bytes=64)
        x_scales = keep.tile([P, N_WINDOWS, PASSES, P], U8, align_bytes=64)

        def prepare_x(w):
            x_pairs = pairs_pool.tile([P, PASSES, P, 2], F32, align_bytes=64)
            transpose_rows(x_rows[w][:], x_pairs[:], nc.scalar.copy)
            nc.vector.quantize_mx(
                out=x_codes[:, w, :, :].rearrange("p c r -> p (c r)").bitcast(FP8X4),
                scales=x_scales[:, w, :, :].rearrange("p c r -> p (c r)"),
                in_=x_pairs[:].rearrange("p c r u -> p (c r u)").bitcast(BF16),
            )

        def weight_tiles(label):
            codes = keep.tile([P, PASSES, FEATURES], U32, name=label + "_codes", align_bytes=64)
            scales = keep.tile([P, PASSES, FEATURES], U8, name=label + "_scales", align_bytes=64)
            return codes, scales

        def prepare_weight_pair(rows, tiles, q):
            codes, scales = tiles
            w_pairs = pairs_pool.tile([P, PASSES, 2 * P, 2], F32, align_bytes=64)
            transpose_rows(rows[:, q, 0, :], w_pairs[:, :, 0:P, :], nc.scalar.copy)
            transpose_rows(rows[:, q, 1, :], w_pairs[:, :, P : 2 * P, :], nc.vector.tensor_copy)
            cols = slice(2 * P * q, 2 * P * (q + 1))
            for c in range(PASSES):
                nc.vector.quantize_mx(
                    out=codes[:, c, cols].bitcast(FP8X4),
                    scales=scales[:, c, cols],
                    in_=w_pairs[:, c, :, :].rearrange("p n u -> p (n u)").bitcast(BF16),
                )

        def prepare_weight_half(rows, tiles, half):
            for q in range(half * PAIRS_PER_HALF, (half + 1) * PAIRS_PER_HALF):
                prepare_weight_pair(rows, tiles, q)

        wv_tiles = weight_tiles("wv")
        wo_tiles = weight_tiles("wo")

        def product(acc, left_codes, left_scales, tiles, half):
            codes, scales = tiles
            cols = slice(half * N_TILE, (half + 1) * N_TILE)
            for c in range(PASSES):
                nc.tensor.matmul_mx(
                    out=acc,
                    lhsT=left_codes[c].bitcast(FP8X4),
                    lhsT_scale=left_scales[c],
                    rhs=codes[:, c, cols].bitcast(FP8X4),
                    rhs_scale=scales[:, c, cols],
                    start=(c == 0),
                    stop=(c == PASSES - 1),
                )

        bv_all = keep.tile([P, FEATURES], F32)
        bo_all = keep.tile([P, FEATURES], F32)

        def spread_biases():
            for half in range(HALVES):
                cols = slice(half * N_TILE, (half + 1) * N_TILE)
                bv_acc = psum.tile([P, N_TILE], F32, tag="acc")
                nc.tensor.matmul(
                    out=bv_acc[:], lhsT=ones[:], rhs=bias_rows["bv"][:, cols], start=True, stop=True
                )
                nc.scalar.copy(
                    out=bv_all[:, cols].rearrange("p (u e m) -> p u e m", u=2, e=2),
                    in_=bv_acc[:].rearrange("p (u m e) -> p u e m", u=2, e=2),
                )
                bo_acc = psum.tile([P, N_TILE], F32, tag="acc")
                nc.tensor.matmul(
                    out=bo_acc[:], lhsT=ones[:], rhs=bias_rows["bo"][:, cols], start=True, stop=True
                )
                nc.vector.tensor_copy(out=bo_all[:, cols], in_=bo_acc[:])

        xw_rows = {}

        def project_xw(w, half):
            xw_acc = psum.tile([P, N_TILE], F32, tag="acc")
            product(
                xw_acc[:],
                [x_codes[:, w, c, :] for c in range(PASSES)],
                [x_scales[:, w, c, :] for c in range(PASSES)],
                wv_tiles,
                half,
            )
            xw_half = xw_pool.tile([P, N_TILE], F32)
            copy = nc.scalar.copy if w % 2 == 0 else nc.vector.tensor_copy
            copy(out=xw_half[:], in_=xw_acc[:])
            xw_rows[w, half] = xw_half

        ctx_rows = {}

        def mix(w):
            ctx_win = ctx_pool.tile([P, FEATURES], BF16)
            for half in range(HALVES):
                cols = slice(half * N_TILE, (half + 1) * N_TILE)
                mix_acc = psum.tile([P, N_TILE], F32, tag="acc")
                nc.tensor.matmul(
                    out=mix_acc[:],
                    lhsT=band_t[:, w, :],
                    rhs=xw_rows[w, half][:],
                    start=True,
                    stop=True,
                )
                nc.vector.scalar_tensor_tensor(
                    out=ctx_win[:, cols],
                    in0=bv_all[:, cols],
                    scalar=tap_sums[:, w : w + 1],
                    in1=mix_acc[:],
                    op0=MULT,
                    op1=ADD,
                )
            ctx_rows[w] = ctx_win

        ctx_quads = keep.tile([P, PASSES, TOKENS, PACK], BF16, align_bytes=64)
        ctx_codes = keep.tile([P, PASSES, TOKENS], U32, align_bytes=64)
        ctx_scales = keep.tile([P, PASSES, TOKENS], U8, align_bytes=64)

        def flip_ctx(w):
            first, lo, hi = window_place(w)
            for c in range(PASSES):
                flipped = psum.tile([P, PACK, P], BF16, tag="flipped")
                for t in range(PACK):
                    blk = c * PACK + t
                    nc.tensor.transpose(
                        flipped[:, t, :], ctx_rows[w][:, blk * P : (blk + 1) * P], ident_bf[:]
                    )
                nc.scalar.copy(
                    out=ctx_quads[:, c, first + lo : first + hi, :],
                    in_=flipped[:, :, lo:hi].rearrange("p t i -> p i t"),
                )

        def quantise_ctx(tb):
            tokens = slice(tb * P, (tb + 1) * P)
            for c in range(PASSES):
                nc.vector.quantize_mx(
                    out=ctx_codes[:, c, tokens].bitcast(FP8X4),
                    scales=ctx_scales[:, c, tokens],
                    in_=ctx_quads[:, c, tokens, :].rearrange("p i t -> p (i t)"),
                )

        def project_out(tb):
            tokens = slice(tb * P, (tb + 1) * P)
            for half in range(HALVES):
                cols = slice(half * N_TILE, (half + 1) * N_TILE)
                out_acc = psum.tile([P, N_TILE], F32, tag="acc")
                product(
                    out_acc[:],
                    [ctx_codes[:, c, tokens] for c in range(PASSES)],
                    [ctx_scales[:, c, tokens] for c in range(PASSES)],
                    wo_tiles,
                    half,
                )
                out_sb = out_pool.tile([P, N_TILE], F32)
                nc.vector.tensor_tensor(out=out_sb[:], in0=out_acc[:], in1=bo_all[:, cols], op=ADD)
                nc.sync.dma_start(out=out_hbm[tokens, cols], in_=out_sb[:])

        prepare_x(0)
        spread_biases()
        prepare_weight_half(wv_rows, wv_tiles, 0)
        for w in range(1, ROUND):
            prepare_x(w)
        for first_w in range(0, N_WINDOWS, ROUND):
            for w in range(first_w + ROUND, min(first_w + 2 * ROUND, N_WINDOWS)):
                prepare_x(w)
            if first_w + ROUND >= N_WINDOWS:
                prepare_weight_half(wv_rows, wv_tiles, 1)
                prepare_band()
            for w in range(first_w, min(first_w + ROUND, N_WINDOWS)):
                project_xw(w, 0)
        for w in range(N_WINDOWS):
            project_xw(w, 1)

        for w in range(N_WINDOWS + 1):
            if w < N_WINDOWS:
                mix(w)
            if w >= 2:
                project_out(w - 2)
            if w < HALVES:
                prepare_weight_half(wo_rows, wo_tiles, w)
            if w < N_WINDOWS:
                flip_ctx(w)
            if 1 <= w < N_WINDOWS:
                quantise_ctx(w - 1)
